import numpy as np
import ml_dtypes

BF16 = ml_dtypes.bfloat16


def bf(x):
    return np.asarray(x, np.float32).astype(BF16)


def f32(x):
    return np.asarray(x, np.float32)


def f64(x):
    return np.asarray(x).astype(np.float64)


def striped(idx):
    return np.tile(idx.reshape(-1, 16).T, (8, 1))


C, E, S, N, B, M, T = 512, 256, 4096, 4096, 8, 64, 8
PAD = 0
SA, SC = 0.3, 0.5


def setup_inputs():
    x = np.random.standard_normal((C, S))
    x[:E] *= SA
    x[E:] *= SC
    x[:, PAD] = 0.0
    return {"x": f32(x), "offs": striped(np.random.permutation(np.tile(np.arange(S), 2))[:N])}


def reference(x, offs):
    idx = offs[:16].T.reshape(-1)
    bag = f64(x)[:, idx].reshape(C, T, B, M).sum(axis=1)
    ma, mc = bag[:E], bag[E:]
    q = ma.sum(axis=2) / M
    p = (ma * q[:, :, None]).sum(axis=0)
    w = np.exp(p)
    attn = w / w.sum(axis=1, keepdims=True)
    return (mc * attn[None, :, :]).sum(axis=2)

@@ -1,0 +1,97 @@
+import concourse.mybir as mybir
+
+F32 = mybir.dt.float32
+BF16 = mybir.dt.bfloat16
+U16 = mybir.dt.uint16
+ADD = mybir.AluOpType.add
+MULT = mybir.AluOpType.mult
+MAX = mybir.AluOpType.max
+EXP = mybir.ActivationFunctionType.Exp
+INNERMOST = mybir.AxisListType.X
+
+P = 128
+VOCAB = 4096
+WORDS, DIALOGUES, SLOTS = 8, 8, 64
+PIECE = DIALOGUES * SLOTS
+PIECE_COLUMNS = PIECE // 16
+QUERY_BLOCKS = 2
+VALUE_BLOCKS = 2
+
+FLOPS = 512 * (WORDS - 1) * PIECE + 256 * PIECE + 2 * 256 * PIECE + 2 * 256 * PIECE
+
+
+def by_dialogue(flat):
+    return flat.rearrange("p (b m) -> p b m", m=SLOTS)
+
+
+def tile_encoder_kernel(tc, x, offs, out):
+    nc = tc.nc
+    with (
+        tc.tile_pool(name="held", bufs=1) as held,
+        tc.psum_pool(name="psum", bufs=1) as psum,
+    ):
+        offsets = held.tile([P, WORDS * PIECE_COLUMNS], U16, name="offsets")
+        nc.sync.dma_start(offsets[:], offs)
+        tables = []
+        for k in range(QUERY_BLOCKS + VALUE_BLOCKS):
+            table = held.tile([P, VOCAB], F32, name=f"table{k}")
+            nc.sync.dma_start(table[:], x[k * P : (k + 1) * P, :])
+            tables.append(table)
+
+        ones = held.tile([P, P], BF16, name="ones")
+        nc.vector.memset(ones[:], 1.0)
+
+        def gather_bag(k):
+            sums = [held.tile([P, PIECE], F32, name=f"sum{k}_{i}") for i in range(2)]
+            for t in range(WORDS):
+                picked = tables[k][:].indirect(offsets[:, t * PIECE_COLUMNS : (t + 1) * PIECE_COLUMNS])
+                if t == 0:
+                    nc.vector.tensor_copy(sums[0][:], picked)
+                else:
+                    nc.vector.tensor_tensor(sums[t % 2][:], picked, sums[(t - 1) % 2][:], ADD)
+            return sums[(WORDS - 1) % 2]
+
+        scores = psum.tile([P, PIECE], F32, name="scores")
+        for k in range(QUERY_BLOCKS):
+            bag = gather_bag(k)
+            slot_sum = held.tile([P, DIALOGUES], F32, name=f"slot_sum{k}")
+            nc.vector.tensor_reduce(slot_sum[:], by_dialogue(bag[:]), INNERMOST, ADD)
+            products = held.tile([P, PIECE], BF16, name=f"products{k}")
+            nc.vector.scalar_tensor_tensor(
+                by_dialogue(products[:]),
+                by_dialogue(bag[:]),
+                1.0 / SLOTS,
+                slot_sum[:].unsqueeze(2).to_broadcast([P, DIALOGUES, SLOTS]),
+                MULT,
+                MULT,
+            )
+            nc.tensor.matmul(scores[:], ones[:], products[:], start=(k == 0), stop=(k == QUERY_BLOCKS - 1))
+
+        value_bags = [gather_bag(QUERY_BLOCKS)]
+
+        negative_max = held.tile([P, DIALOGUES], F32, name="negative_max")
+        nc.vector.tensor_reduce(negative_max[:], by_dialogue(scores[:]), INNERMOST, MAX, negate=True)
+        weights = held.tile([P, PIECE], F32, name="weights")
+        weight_sum = held.tile([P, DIALOGUES], F32, name="weight_sum")
+        for b in range(DIALOGUES):
+            slots = slice(b * SLOTS, (b + 1) * SLOTS)
+            nc.scalar.activation(
+                weights[:, slots],
+                scores[:, slots],
+                EXP,
+                bias=negative_max[:, b : b + 1],
+                accum_out=weight_sum[:, b : b + 1],
+            )
+        inverse_sum = held.tile([P, DIALOGUES], F32, name="inverse_sum")
+        nc.vector.reciprocal(inverse_sum[:], weight_sum[:])
+
+        value_bags.append(gather_bag(QUERY_BLOCKS + 1))
+
+        for k, bag in enumerate(value_bags):
+            weighted = held.tile([P, PIECE], F32, name=f"weighted{k}")
+            nc.vector.tensor_tensor(weighted[:], bag[:], weights[:], MULT)
+            unscaled = held.tile([P, DIALOGUES], F32, name=f"unscaled{k}")
+            nc.vector.tensor_reduce(unscaled[:], by_dialogue(weighted[:]), INNERMOST, ADD)
+            encoded = held.tile([P, DIALOGUES], F32, name=f"encoded{k}")
+            nc.vector.tensor_tensor(encoded[:], unscaled[:], inverse_sum[:], MULT)
+            nc.sync.dma_start(out[k * P : (k + 1) * P, :], encoded[:])

@@ -7,6 +7,7 @@ ADD = mybir.AluOpType.add
 MULT = mybir.AluOpType.mult
 MAX = mybir.AluOpType.max
 EXP = mybir.ActivationFunctionType.Exp
+COPY = mybir.ActivationFunctionType.Copy
 INNERMOST = mybir.AxisListType.X
 
 P = 128
@@ -54,17 +55,17 @@ def tile_encoder_kernel(tc, x, offs, out):
         scores = psum.tile([P, PIECE], F32, name="scores")
         for k in range(QUERY_BLOCKS):
             bag = gather_bag(k)
-            slot_sum = held.tile([P, DIALOGUES], F32, name=f"slot_sum{k}")
-            nc.vector.tensor_reduce(slot_sum[:], by_dialogue(bag[:]), INNERMOST, ADD)
+            query = held.tile([P, DIALOGUES], F32, name=f"query{k}")
+            unused = held.tile([P, PIECE], BF16, name=f"unused{k}")
             products = held.tile([P, PIECE], BF16, name=f"products{k}")
-            nc.vector.scalar_tensor_tensor(
-                by_dialogue(products[:]),
-                by_dialogue(bag[:]),
-                1.0 / SLOTS,
-                slot_sum[:].unsqueeze(2).to_broadcast([P, DIALOGUES, SLOTS]),
-                MULT,
-                MULT,
-            )
+            for b in range(DIALOGUES):
+                slots = slice(b * SLOTS, (b + 1) * SLOTS)
+                nc.scalar.activation(
+                    unused[:, slots], bag[:, slots], COPY, scale=1.0 / SLOTS, accum_out=query[:, b : b + 1]
+                )
+            for b in range(DIALOGUES):
+                slots = slice(b * SLOTS, (b + 1) * SLOTS)
+                nc.scalar.activation(products[:, slots], bag[:, slots], COPY, scale=query[:, b : b + 1])
             nc.tensor.matmul(scores[:], ones[:], products[:], start=(k == 0), stop=(k == QUERY_BLOCKS - 1))
 
         value_bags = [gather_bag(QUERY_BLOCKS)]

@@ -83,10 +83,10 @@ def tile_encoder_kernel(tc, x, offs, out):
                 bias=negative_max[:, b : b + 1],
                 accum_out=weight_sum[:, b : b + 1],
             )
-        inverse_sum = held.tile([P, DIALOGUES], F32, name="inverse_sum")
-        nc.vector.reciprocal(inverse_sum[:], weight_sum[:])
 
         value_bags.append(gather_bag(QUERY_BLOCKS + 1))
+        inverse_sum = held.tile([P, DIALOGUES], F32, name="inverse_sum")
+        nc.vector.reciprocal(inverse_sum[:], weight_sum[:])
 
         for k, bag in enumerate(value_bags):
             weighted = held.tile([P, PIECE], F32, name=f"weighted{k}")

@@ -15,6 +15,7 @@ VOCAB = 4096
 WORDS, DIALOGUES, SLOTS = 8, 8, 64
 PIECE = DIALOGUES * SLOTS
 PIECE_COLUMNS = PIECE // 16
+HALF_PIECE = PIECE // 2
 QUERY_BLOCKS = 2
 VALUE_BLOCKS = 2
 
@@ -44,12 +45,13 @@ def tile_encoder_kernel(tc, x, offs, out):
 
         def gather_bag(k):
             sums = [held.tile([P, PIECE], F32, name=f"sum{k}_{i}") for i in range(2)]
-            for t in range(WORDS):
-                picked = tables[k][:].indirect(offsets[:, t * PIECE_COLUMNS : (t + 1) * PIECE_COLUMNS])
-                if t == 0:
-                    nc.vector.tensor_copy(sums[0][:], picked)
-                else:
-                    nc.vector.tensor_tensor(sums[t % 2][:], picked, sums[(t - 1) % 2][:], ADD)
+            nc.vector.tensor_copy(sums[0][:], tables[k][:].indirect(offsets[:, 0:PIECE_COLUMNS]))
+            for t in range(1, WORDS):
+                for h in range(2):
+                    entries = slice(h * HALF_PIECE, (h + 1) * HALF_PIECE)
+                    first_column = (t * PIECE + h * HALF_PIECE) // 16
+                    picked = tables[k][:].indirect(offsets[:, first_column : first_column + HALF_PIECE // 16])
+                    nc.vector.tensor_tensor(sums[t % 2][:, entries], picked, sums[(t - 1) % 2][:, entries], ADD)
             return sums[(WORDS - 1) % 2]
 
         scores = psum.tile([P, PIECE], F32, name="scores")

@@ -13,17 +13,22 @@ INNERMOST = mybir.AxisListType.X
 P = 128
 VOCAB = 4096
 WORDS, DIALOGUES, SLOTS = 8, 8, 64
+HALF = WORDS // 2
 PIECE = DIALOGUES * SLOTS
 PIECE_COLUMNS = PIECE // 16
-HALF_PIECE = PIECE // 2
-QUERY_BLOCKS = 2
-VALUE_BLOCKS = 2
+QUERY_BLOCKS = (0, 1)
+VALUE_BLOCKS = (2, 3)
+BLOCKS = QUERY_BLOCKS + VALUE_BLOCKS
 
 FLOPS = 512 * (WORDS - 1) * PIECE + 256 * PIECE + 2 * 256 * PIECE + 2 * 256 * PIECE
 
 
 def by_dialogue(flat):
     return flat.rearrange("p (b m) -> p b m", m=SLOTS)
+
+
+def slots_of(b):
+    return slice(b * SLOTS, (b + 1) * SLOTS)
 
 
 def tile_encoder_kernel(tc, x, offs, out):
@@ -34,67 +39,100 @@ def tile_encoder_kernel(tc, x, offs, out):
     ):
         offsets = held.tile([P, WORDS * PIECE_COLUMNS], U16, name="offsets")
         nc.sync.dma_start(offsets[:], offs)
+
         tables = []
-        for k in range(QUERY_BLOCKS + VALUE_BLOCKS):
+        for k in BLOCKS:
             table = held.tile([P, VOCAB], F32, name=f"table{k}")
-            nc.sync.dma_start(table[:], x[k * P : (k + 1) * P, :])
+            nc.sync.dma_start(table[:, : VOCAB // 2], x[k * P : (k + 1) * P, : VOCAB // 2])
+            nc.scalar.dma_start(table[:, VOCAB // 2 :], x[k * P : (k + 1) * P, VOCAB // 2 :])
             tables.append(table)
 
         ones = held.tile([P, P], BF16, name="ones")
         nc.vector.memset(ones[:], 1.0)
 
-        def gather_bag(k):
-            sums = [held.tile([P, PIECE], F32, name=f"sum{k}_{i}") for i in range(2)]
-            nc.vector.tensor_copy(sums[0][:], tables[k][:].indirect(offsets[:, 0:PIECE_COLUMNS]))
-            for t in range(1, WORDS):
-                for h in range(2):
-                    entries = slice(h * HALF_PIECE, (h + 1) * HALF_PIECE)
-                    first_column = (t * PIECE + h * HALF_PIECE) // 16
-                    picked = tables[k][:].indirect(offsets[:, first_column : first_column + HALF_PIECE // 16])
-                    nc.vector.tensor_tensor(sums[t % 2][:, entries], picked, sums[(t - 1) % 2][:, entries], ADD)
-            return sums[(WORDS - 1) % 2]
+        sums = [[held.tile([P, PIECE], F32, name=f"sum{k}_{i}") for i in range(2)] for k in BLOCKS]
+        bags = [sums[k][(WORDS - 1) % 2] for k in BLOCKS]
+
+        def look_up(k, t):
+            picked = tables[k][:].indirect(offsets[:, t * PIECE_COLUMNS : (t + 1) * PIECE_COLUMNS])
+            if t == 0:
+                nc.vector.tensor_copy(sums[k][0][:], picked)
+            else:
+                nc.vector.tensor_tensor(sums[k][t % 2][:], picked, sums[k][(t - 1) % 2][:], ADD)
+
+        def finish_one_start_next(k, steps):
+            for t in steps:
+                look_up(k, HALF + t)
+                look_up(k + 1, t)
 
         scores = psum.tile([P, PIECE], F32, name="scores")
-        for k in range(QUERY_BLOCKS):
-            bag = gather_bag(k)
+
+        def add_to_scores(k):
             query = held.tile([P, DIALOGUES], F32, name=f"query{k}")
-            unused = held.tile([P, PIECE], BF16, name=f"unused{k}")
+            discarded = held.tile([P, PIECE], BF16, name=f"discarded{k}")
             products = held.tile([P, PIECE], BF16, name=f"products{k}")
             for b in range(DIALOGUES):
-                slots = slice(b * SLOTS, (b + 1) * SLOTS)
                 nc.scalar.activation(
-                    unused[:, slots], bag[:, slots], COPY, scale=1.0 / SLOTS, accum_out=query[:, b : b + 1]
+                    discarded[:, slots_of(b)],
+                    bags[k][:, slots_of(b)],
+                    COPY,
+                    scale=1.0 / SLOTS,
+                    accum_out=query[:, b : b + 1],
                 )
             for b in range(DIALOGUES):
-                slots = slice(b * SLOTS, (b + 1) * SLOTS)
-                nc.scalar.activation(products[:, slots], bag[:, slots], COPY, scale=query[:, b : b + 1])
-            nc.tensor.matmul(scores[:], ones[:], products[:], start=(k == 0), stop=(k == QUERY_BLOCKS - 1))
+                nc.scalar.activation(
+                    products[:, slots_of(b)], bags[k][:, slots_of(b)], COPY, scale=query[:, b : b + 1]
+                )
+            nc.tensor.matmul(
+                scores[:], ones[:], products[:], start=(k == QUERY_BLOCKS[0]), stop=(k == QUERY_BLOCKS[-1])
+            )
 
-        value_bags = [gather_bag(QUERY_BLOCKS)]
+        for t in range(HALF):
+            look_up(BLOCKS[0], t)
+        for k in QUERY_BLOCKS:
+            finish_one_start_next(k, range(HALF))
+            add_to_scores(k)
 
+        first_value, last_value = VALUE_BLOCKS
+        finish_one_start_next(first_value, range(HALF // 2))
         negative_max = held.tile([P, DIALOGUES], F32, name="negative_max")
         nc.vector.tensor_reduce(negative_max[:], by_dialogue(scores[:]), INNERMOST, MAX, negate=True)
         weights = held.tile([P, PIECE], F32, name="weights")
         weight_sum = held.tile([P, DIALOGUES], F32, name="weight_sum")
         for b in range(DIALOGUES):
-            slots = slice(b * SLOTS, (b + 1) * SLOTS)
             nc.scalar.activation(
-                weights[:, slots],
-                scores[:, slots],
+                weights[:, slots_of(b)],
+                scores[:, slots_of(b)],
                 EXP,
                 bias=negative_max[:, b : b + 1],
                 accum_out=weight_sum[:, b : b + 1],
             )
+        finish_one_start_next(first_value, range(HALF // 2, HALF))
 
-        value_bags.append(gather_bag(QUERY_BLOCKS + 1))
         inverse_sum = held.tile([P, DIALOGUES], F32, name="inverse_sum")
-        nc.vector.reciprocal(inverse_sum[:], weight_sum[:])
+        weighted = {k: held.tile([P, PIECE], F32, name=f"weighted{k}") for k in VALUE_BLOCKS}
+        unscaled = {k: held.tile([P, DIALOGUES], F32, name=f"unscaled{k}") for k in VALUE_BLOCKS}
+        encoded = {k: held.tile([P, DIALOGUES], F32, name=f"encoded{k}") for k in VALUE_BLOCKS}
 
-        for k, bag in enumerate(value_bags):
-            weighted = held.tile([P, PIECE], F32, name=f"weighted{k}")
-            nc.vector.tensor_tensor(weighted[:], bag[:], weights[:], MULT)
-            unscaled = held.tile([P, DIALOGUES], F32, name=f"unscaled{k}")
-            nc.vector.tensor_reduce(unscaled[:], by_dialogue(weighted[:]), INNERMOST, ADD)
-            encoded = held.tile([P, DIALOGUES], F32, name=f"encoded{k}")
-            nc.vector.tensor_tensor(encoded[:], unscaled[:], inverse_sum[:], MULT)
-            nc.sync.dma_start(out[k * P : (k + 1) * P, :], encoded[:])
+        def weigh(k):
+            nc.vector.tensor_tensor(weighted[k][:], bags[k][:], weights[:], MULT)
+
+        def sum_slots(k):
+            nc.vector.tensor_reduce(unscaled[k][:], by_dialogue(weighted[k][:]), INNERMOST, ADD)
+
+        def normalise_and_store(k):
+            nc.vector.tensor_tensor(encoded[k][:], unscaled[k][:], inverse_sum[:], MULT)
+            first_row = (k - first_value) * P
+            nc.sync.dma_start(out[first_row : first_row + P, :], encoded[k][:])
+
+        look_up(last_value, HALF)
+        weigh(first_value)
+        look_up(last_value, HALF + 1)
+        sum_slots(first_value)
+        look_up(last_value, HALF + 2)
+        nc.vector.reciprocal(inverse_sum[:], weight_sum[:])
+        look_up(last_value, HALF + 3)
+        normalise_and_store(first_value)
+        weigh(last_value)
+        sum_slots(last_value)
+        normalise_and_store(last_value)

@@ -13,9 +13,7 @@ INNERMOST = mybir.AxisListType.X
 P = 128
 VOCAB = 4096
 WORDS, DIALOGUES, SLOTS = 8, 8, 64
-HALF = WORDS // 2
 PIECE = DIALOGUES * SLOTS
-PIECE_COLUMNS = PIECE // 16
 QUERY_BLOCKS = (0, 1)
 VALUE_BLOCKS = (2, 3)
 BLOCKS = QUERY_BLOCKS + VALUE_BLOCKS
@@ -37,7 +35,7 @@ def tile_encoder_kernel(tc, x, offs, out):
         tc.tile_pool(name="held", bufs=1) as held,
         tc.psum_pool(name="psum", bufs=1) as psum,
     ):
-        offsets = held.tile([P, WORDS * PIECE_COLUMNS], U16, name="offsets")
+        offsets = held.tile([P, WORDS * PIECE // 16], U16, name="offsets")
         nc.sync.dma_start(offsets[:], offs)
 
         tables = []
@@ -53,17 +51,14 @@ def tile_encoder_kernel(tc, x, offs, out):
         sums = [[held.tile([P, PIECE], F32, name=f"sum{k}_{i}") for i in range(2)] for k in BLOCKS]
         bags = [sums[k][(WORDS - 1) % 2] for k in BLOCKS]
 
-        def look_up(k, t):
-            picked = tables[k][:].indirect(offsets[:, t * PIECE_COLUMNS : (t + 1) * PIECE_COLUMNS])
+        def look_up(k, t, first=0, width=PIECE):
+            entries = slice(first, first + width)
+            first_column = (t * PIECE + first) // 16
+            picked = tables[k][:].indirect(offsets[:, first_column : first_column + width // 16])
             if t == 0:
-                nc.vector.tensor_copy(sums[k][0][:], picked)
+                nc.vector.tensor_copy(sums[k][0][:, entries], picked)
             else:
-                nc.vector.tensor_tensor(sums[k][t % 2][:], picked, sums[k][(t - 1) % 2][:], ADD)
-
-        def finish_one_start_next(k, steps):
-            for t in steps:
-                look_up(k, HALF + t)
-                look_up(k + 1, t)
+                nc.vector.tensor_tensor(sums[k][t % 2][:, entries], picked, sums[k][(t - 1) % 2][:, entries], ADD)
 
         scores = psum.tile([P, PIECE], F32, name="scores")
 
@@ -87,14 +82,17 @@ def tile_encoder_kernel(tc, x, offs, out):
                 scores[:], ones[:], products[:], start=(k == QUERY_BLOCKS[0]), stop=(k == QUERY_BLOCKS[-1])
             )
 
-        for t in range(HALF):
-            look_up(BLOCKS[0], t)
         for k in QUERY_BLOCKS:
-            finish_one_start_next(k, range(HALF))
+            look_up(k, 0)
+            for t in range(1, WORDS):
+                for first in (0, PIECE // 2):
+                    look_up(k, t, first, PIECE // 2)
             add_to_scores(k)
 
-        first_value, last_value = VALUE_BLOCKS
-        finish_one_start_next(first_value, range(HALF // 2))
+        for t in range(WORDS // 2):
+            for k in VALUE_BLOCKS:
+                look_up(k, t)
+
         negative_max = held.tile([P, DIALOGUES], F32, name="negative_max")
         nc.vector.tensor_reduce(negative_max[:], by_dialogue(scores[:]), INNERMOST, MAX, negate=True)
         weights = held.tile([P, PIECE], F32, name="weights")
@@ -107,32 +105,21 @@ def tile_encoder_kernel(tc, x, offs, out):
                 bias=negative_max[:, b : b + 1],
                 accum_out=weight_sum[:, b : b + 1],
             )
-        finish_one_start_next(first_value, range(HALF // 2, HALF))
+
+        for t in range(WORDS // 2, WORDS):
+            for k in VALUE_BLOCKS:
+                look_up(k, t)
 
         inverse_sum = held.tile([P, DIALOGUES], F32, name="inverse_sum")
+        nc.vector.reciprocal(inverse_sum[:], weight_sum[:])
         weighted = {k: held.tile([P, PIECE], F32, name=f"weighted{k}") for k in VALUE_BLOCKS}
         unscaled = {k: held.tile([P, DIALOGUES], F32, name=f"unscaled{k}") for k in VALUE_BLOCKS}
         encoded = {k: held.tile([P, DIALOGUES], F32, name=f"encoded{k}") for k in VALUE_BLOCKS}
-
-        def weigh(k):
+        for k in VALUE_BLOCKS:
             nc.vector.tensor_tensor(weighted[k][:], bags[k][:], weights[:], MULT)
-
-        def sum_slots(k):
+        for k in VALUE_BLOCKS:
             nc.vector.tensor_reduce(unscaled[k][:], by_dialogue(weighted[k][:]), INNERMOST, ADD)
-
-        def normalise_and_store(k):
+        for k in VALUE_BLOCKS:
             nc.vector.tensor_tensor(encoded[k][:], unscaled[k][:], inverse_sum[:], MULT)
-            first_row = (k - first_value) * P
+            first_row = (k - VALUE_BLOCKS[0]) * P
             nc.sync.dma_start(out[first_row : first_row + P, :], encoded[k][:])
-
-        look_up(last_value, HALF)
-        weigh(first_value)
-        look_up(last_value, HALF + 1)
-        sum_slots(first_value)
-        look_up(last_value, HALF + 2)
-        nc.vector.reciprocal(inverse_sum[:], weight_sum[:])
-        look_up(last_value, HALF + 3)
-        normalise_and_store(first_value)
-        weigh(last_value)
-        sum_slots(last_value)
-        normalise_and_store(last_value)

@@ -37,12 +37,10 @@ def tile_encoder_kernel(tc, x, offs, out):
     ):
         offsets = held.tile([P, WORDS * PIECE // 16], U16, name="offsets")
         nc.sync.dma_start(offsets[:], offs)
-
         tables = []
         for k in BLOCKS:
             table = held.tile([P, VOCAB], F32, name=f"table{k}")
-            nc.sync.dma_start(table[:, : VOCAB // 2], x[k * P : (k + 1) * P, : VOCAB // 2])
-            nc.scalar.dma_start(table[:, VOCAB // 2 :], x[k * P : (k + 1) * P, VOCAB // 2 :])
+            nc.sync.dma_start(table[:], x[k * P : (k + 1) * P, :])
             tables.append(table)
 
         ones = held.tile([P, P], BF16, name="ones")
@@ -51,7 +49,7 @@ def tile_encoder_kernel(tc, x, offs, out):
         sums = [[held.tile([P, PIECE], F32, name=f"sum{k}_{i}") for i in range(2)] for k in BLOCKS]
         bags = [sums[k][(WORDS - 1) % 2] for k in BLOCKS]
 
-        def look_up(k, t, first=0, width=PIECE):
+        def look_up(k, t, first, width):
             entries = slice(first, first + width)
             first_column = (t * PIECE + first) // 16
             picked = tables[k][:].indirect(offsets[:, first_column : first_column + width // 16])
@@ -60,9 +58,15 @@ def tile_encoder_kernel(tc, x, offs, out):
             else:
                 nc.vector.tensor_tensor(sums[k][t % 2][:, entries], picked, sums[k][(t - 1) % 2][:, entries], ADD)
 
-        scores = psum.tile([P, PIECE], F32, name="scores")
+        def sum_bag(k):
+            look_up(k, 0, 0, PIECE)
+            for t in range(1, WORDS):
+                for first in (0, PIECE // 2):
+                    look_up(k, t, first, PIECE // 2)
 
-        def add_to_scores(k):
+        scores = psum.tile([P, PIECE], F32, name="scores")
+        for k in QUERY_BLOCKS:
+            sum_bag(k)
             query = held.tile([P, DIALOGUES], F32, name=f"query{k}")
             discarded = held.tile([P, PIECE], BF16, name=f"discarded{k}")
             products = held.tile([P, PIECE], BF16, name=f"products{k}")
@@ -82,17 +86,7 @@ def tile_encoder_kernel(tc, x, offs, out):
                 scores[:], ones[:], products[:], start=(k == QUERY_BLOCKS[0]), stop=(k == QUERY_BLOCKS[-1])
             )
 
-        for k in QUERY_BLOCKS:
-            look_up(k, 0)
-            for t in range(1, WORDS):
-                for first in (0, PIECE // 2):
-                    look_up(k, t, first, PIECE // 2)
-            add_to_scores(k)
-
-        for t in range(WORDS // 2):
-            for k in VALUE_BLOCKS:
-                look_up(k, t)
-
+        sum_bag(VALUE_BLOCKS[0])
         negative_max = held.tile([P, DIALOGUES], F32, name="negative_max")
         nc.vector.tensor_reduce(negative_max[:], by_dialogue(scores[:]), INNERMOST, MAX, negate=True)
         weights = held.tile([P, PIECE], F32, name="weights")
@@ -105,10 +99,7 @@ def tile_encoder_kernel(tc, x, offs, out):
                 bias=negative_max[:, b : b + 1],
                 accum_out=weight_sum[:, b : b + 1],
             )
-
-        for t in range(WORDS // 2, WORDS):
-            for k in VALUE_BLOCKS:
-                look_up(k, t)
+        sum_bag(VALUE_BLOCKS[1])
 
         inverse_sum = held.tile([P, DIALOGUES], F32, name="inverse_sum")
         nc.vector.reciprocal(inverse_sum[:], weight_sum[:])

@@ -99,18 +99,43 @@ def tile_encoder_kernel(tc, x, offs, out):
                 bias=negative_max[:, b : b + 1],
                 accum_out=weight_sum[:, b : b + 1],
             )
-        sum_bag(VALUE_BLOCKS[1])
-
         inverse_sum = held.tile([P, DIALOGUES], F32, name="inverse_sum")
         nc.vector.reciprocal(inverse_sum[:], weight_sum[:])
+        attention = held.tile([P, PIECE], F32, name="attention")
+        for b in range(DIALOGUES):
+            nc.scalar.activation(
+                attention[:, slots_of(b)], weights[:, slots_of(b)], COPY, scale=inverse_sum[:, b : b + 1]
+            )
+
         weighted = {k: held.tile([P, PIECE], F32, name=f"weighted{k}") for k in VALUE_BLOCKS}
-        unscaled = {k: held.tile([P, DIALOGUES], F32, name=f"unscaled{k}") for k in VALUE_BLOCKS}
         encoded = {k: held.tile([P, DIALOGUES], F32, name=f"encoded{k}") for k in VALUE_BLOCKS}
-        for k in VALUE_BLOCKS:
-            nc.vector.tensor_tensor(weighted[k][:], bags[k][:], weights[:], MULT)
-        for k in VALUE_BLOCKS:
-            nc.vector.tensor_reduce(unscaled[k][:], by_dialogue(weighted[k][:]), INNERMOST, ADD)
-        for k in VALUE_BLOCKS:
-            nc.vector.tensor_tensor(encoded[k][:], unscaled[k][:], inverse_sum[:], MULT)
+
+        def store(k):
             first_row = (k - VALUE_BLOCKS[0]) * P
             nc.sync.dma_start(out[first_row : first_row + P, :], encoded[k][:])
+
+        k = VALUE_BLOCKS[0]
+        nc.vector.tensor_tensor(weighted[k][:], bags[k][:], attention[:], MULT)
+        discarded_weighted = held.tile([P, PIECE], BF16, name="discarded_weighted")
+        for b in range(DIALOGUES):
+            nc.scalar.activation(
+                discarded_weighted[:, slots_of(b)],
+                weighted[k][:, slots_of(b)],
+                COPY,
+                accum_out=encoded[k][:, b : b + 1],
+            )
+        store(k)
+
+        k = VALUE_BLOCKS[1]
+        sum_bag(k)
+        halves = (slice(0, PIECE // 2), slice(PIECE // 2, PIECE))
+        for half in halves:
+            nc.vector.tensor_tensor(weighted[k][:, half], bags[k][:, half], attention[:, half], MULT)
+        for half in halves:
+            nc.vector.tensor_reduce(
+                encoded[k][:, half.start // SLOTS : half.stop // SLOTS],
+                by_dialogue(weighted[k][:, half]),
+                INNERMOST,
+                ADD,
+            )
+        store(k)

@@ -1,4 +1,5 @@
 import concourse.mybir as mybir
+from concourse.masks import make_identity
 
 F32 = mybir.dt.float32
 BF16 = mybir.dt.bfloat16
@@ -17,6 +18,8 @@ PIECE = DIALOGUES * SLOTS
 QUERY_BLOCKS = (0, 1)
 VALUE_BLOCKS = (2, 3)
 BLOCKS = QUERY_BLOCKS + VALUE_BLOCKS
+PAIR = P // SLOTS
+PAIRS = DIALOGUES // PAIR
 
 FLOPS = 512 * (WORDS - 1) * PIECE + 256 * PIECE + 2 * 256 * PIECE + 2 * 256 * PIECE
 
@@ -27,6 +30,10 @@ def by_dialogue(flat):
 
 def slots_of(b):
     return slice(b * SLOTS, (b + 1) * SLOTS)
+
+
+def slots_of_pair(c):
+    return slice(c * P, (c + 1) * P)
 
 
 def tile_encoder_kernel(tc, x, offs, out):
@@ -45,6 +52,10 @@ def tile_encoder_kernel(tc, x, offs, out):
 
         ones = held.tile([P, P], BF16, name="ones")
         nc.vector.memset(ones[:], 1.0)
+        identity = held.tile([P, P], F32, name="identity")
+        make_identity(nc, identity[:])
+        flipped_attention = held.tile([P, DIALOGUES], F32, name="flipped_attention")
+        nc.gpsimd.memset(flipped_attention[:], 0.0)
 
         sums = [[held.tile([P, PIECE], F32, name=f"sum{k}_{i}") for i in range(2)] for k in BLOCKS]
         bags = [sums[k][(WORDS - 1) % 2] for k in BLOCKS]
@@ -86,7 +97,6 @@ def tile_encoder_kernel(tc, x, offs, out):
                 scores[:], ones[:], products[:], start=(k == QUERY_BLOCKS[0]), stop=(k == QUERY_BLOCKS[-1])
             )
 
-        sum_bag(VALUE_BLOCKS[0])
         negative_max = held.tile([P, DIALOGUES], F32, name="negative_max")
         nc.vector.tensor_reduce(negative_max[:], by_dialogue(scores[:]), INNERMOST, MAX, negate=True)
         weights = held.tile([P, PIECE], F32, name="weights")
@@ -107,7 +117,6 @@ def tile_encoder_kernel(tc, x, offs, out):
                 attention[:, slots_of(b)], weights[:, slots_of(b)], COPY, scale=inverse_sum[:, b : b + 1]
             )
 
-        weighted = {k: held.tile([P, PIECE], F32, name=f"weighted{k}") for k in VALUE_BLOCKS}
         encoded = {k: held.tile([P, DIALOGUES], F32, name=f"encoded{k}") for k in VALUE_BLOCKS}
 
         def store(k):
@@ -115,26 +124,39 @@ def tile_encoder_kernel(tc, x, offs, out):
             nc.sync.dma_start(out[first_row : first_row + P, :], encoded[k][:])
 
         k = VALUE_BLOCKS[0]
-        nc.vector.tensor_tensor(weighted[k][:], bags[k][:], attention[:], MULT)
-        discarded_weighted = held.tile([P, PIECE], BF16, name="discarded_weighted")
-        for b in range(DIALOGUES):
-            nc.scalar.activation(
-                discarded_weighted[:, slots_of(b)],
-                weighted[k][:, slots_of(b)],
-                COPY,
-                accum_out=encoded[k][:, b : b + 1],
+        sum_bag(k)
+        flipped_bag_psum = psum.tile([P, PIECE], F32, name="flipped_bag_psum")
+        for c in range(PAIRS):
+            nc.tensor.transpose(flipped_bag_psum[:, slots_of_pair(c)], bags[k][:, slots_of_pair(c)], identity[:])
+        flipped_bag = held.tile([P, PIECE], F32, name="flipped_bag")
+        nc.scalar.copy(flipped_bag[:], flipped_bag_psum[:])
+        attention_column = psum.tile([P, PAIRS], F32, name="attention_column")
+        for c in range(PAIRS):
+            nc.tensor.matmul(
+                attention_column[:, c : c + 1], attention[:, slots_of_pair(c)], identity[:, 0:1], start=True, stop=True
             )
+        for h in range(PAIR):
+            slots_of_half = slice(h * SLOTS, (h + 1) * SLOTS)
+            nc.scalar.copy(flipped_attention[slots_of_half, h::PAIR], attention_column[slots_of_half, :])
+        encoded_psum = psum.tile([P, DIALOGUES], F32, name="encoded_psum")
+        for c in range(PAIRS):
+            pair = slice(c * PAIR, (c + 1) * PAIR)
+            nc.tensor.matmul(
+                encoded_psum[:, pair], flipped_bag[:, slots_of_pair(c)], flipped_attention[:, pair], start=True, stop=True
+            )
+        nc.scalar.copy(encoded[k][:], encoded_psum[:])
         store(k)
 
         k = VALUE_BLOCKS[1]
         sum_bag(k)
+        weighted = held.tile([P, PIECE], F32, name="weighted")
         halves = (slice(0, PIECE // 2), slice(PIECE // 2, PIECE))
         for half in halves:
-            nc.vector.tensor_tensor(weighted[k][:, half], bags[k][:, half], attention[:, half], MULT)
+            nc.vector.tensor_tensor(weighted[:, half], bags[k][:, half], attention[:, half], MULT)
         for half in halves:
             nc.vector.tensor_reduce(
                 encoded[k][:, half.start // SLOTS : half.stop // SLOTS],
-                by_dialogue(weighted[k][:, half]),
+                by_dialogue(weighted[:, half]),
                 INNERMOST,
                 ADD,
             )

@@ -18,6 +18,8 @@ PIECE = DIALOGUES * SLOTS
 QUERY_BLOCKS = (0, 1)
 VALUE_BLOCKS = (2, 3)
 BLOCKS = QUERY_BLOCKS + VALUE_BLOCKS
+LAST_BLOCK = BLOCKS[-1]
+PARITIES = 2
 PAIR = P // SLOTS
 PAIRS = DIALOGUES // PAIR
 
@@ -28,12 +30,20 @@ def by_dialogue(flat):
     return flat.rearrange("p (b m) -> p b m", m=SLOTS)
 
 
+def dialogue_of_both(flat, b):
+    return flat.rearrange("p (a b m) -> p a b m", a=PARITIES, m=SLOTS)[:, :, b : b + 1, :]
+
+
 def slots_of(b):
     return slice(b * SLOTS, (b + 1) * SLOTS)
 
 
-def slots_of_pair(c):
-    return slice(c * P, (c + 1) * P)
+def sum_of(a):
+    return slice(a * PIECE, (a + 1) * PIECE)
+
+
+def slots_of_pair(c, a=0):
+    return slice(a * PIECE + c * P, a * PIECE + (c + 1) * P)
 
 
 def tile_encoder_kernel(tc, x, offs, out):
@@ -52,50 +62,67 @@ def tile_encoder_kernel(tc, x, offs, out):
 
         ones = held.tile([P, P], BF16, name="ones")
         nc.vector.memset(ones[:], 1.0)
+        zeros = held.tile([P, PIECE], F32, name="zeros")
+        nc.vector.memset(zeros[:], 0.0)
         identity = held.tile([P, P], F32, name="identity")
         make_identity(nc, identity[:])
         flipped_attention = held.tile([P, DIALOGUES], F32, name="flipped_attention")
         nc.gpsimd.memset(flipped_attention[:], 0.0)
 
-        sums = [[held.tile([P, PIECE], F32, name=f"sum{k}_{i}") for i in range(2)] for k in BLOCKS]
-        bags = [sums[k][(WORDS - 1) % 2] for k in BLOCKS]
+        span = {k: PIECE if k == LAST_BLOCK else PARITIES * PIECE for k in BLOCKS}
+        steps = {k: WORDS * PIECE // span[k] for k in BLOCKS}
+        sums = [[held.tile([P, span[k]], F32, name=f"sum{k}_{i}") for i in range(2)] for k in BLOCKS]
+        bags = [sums[k][(steps[k] - 1) % 2] for k in BLOCKS]
 
-        def look_up(k, t, first, width):
-            entries = slice(first, first + width)
-            first_column = (t * PIECE + first) // 16
-            picked = tables[k][:].indirect(offsets[:, first_column : first_column + width // 16])
-            if t == 0:
-                nc.vector.tensor_copy(sums[k][0][:, entries], picked)
+        def look_up(k, step, first, width):
+            columns = slice(first, first + width)
+            entry = step * span[k] + first
+            picked = tables[k][:].indirect(offsets[:, entry // 16 : (entry + width) // 16])
+            if entry == 0:
+                nc.vector.tensor_copy(sums[k][0][:, columns], picked)
+            elif step == 0:
+                nc.vector.tensor_tensor(sums[k][0][:, columns], picked, zeros[:], ADD)
             else:
-                nc.vector.tensor_tensor(sums[k][t % 2][:, entries], picked, sums[k][(t - 1) % 2][:, entries], ADD)
+                nc.vector.tensor_tensor(
+                    sums[k][step % 2][:, columns], picked, sums[k][(step - 1) % 2][:, columns], ADD
+                )
 
         def sum_bag(k):
-            look_up(k, 0, 0, PIECE)
-            for t in range(1, WORDS):
-                for first in (0, PIECE // 2):
-                    look_up(k, t, first, PIECE // 2)
+            for first in range(0, span[k], PIECE):
+                look_up(k, 0, first, PIECE)
+            for step in range(1, steps[k]):
+                for first in (0, span[k] // 2):
+                    look_up(k, step, first, span[k] // 2)
 
         scores = psum.tile([P, PIECE], F32, name="scores")
         for k in QUERY_BLOCKS:
             sum_bag(k)
             query = held.tile([P, DIALOGUES], F32, name=f"query{k}")
-            discarded = held.tile([P, PIECE], BF16, name=f"discarded{k}")
-            products = held.tile([P, PIECE], BF16, name=f"products{k}")
+            discarded = held.tile([P, PARITIES * PIECE], BF16, name=f"discarded{k}")
+            products = held.tile([P, PARITIES * PIECE], BF16, name=f"products{k}")
             for b in range(DIALOGUES):
                 nc.scalar.activation(
-                    discarded[:, slots_of(b)],
-                    bags[k][:, slots_of(b)],
+                    dialogue_of_both(discarded[:], b),
+                    dialogue_of_both(bags[k][:], b),
                     COPY,
                     scale=1.0 / SLOTS,
                     accum_out=query[:, b : b + 1],
                 )
             for b in range(DIALOGUES):
                 nc.scalar.activation(
-                    products[:, slots_of(b)], bags[k][:, slots_of(b)], COPY, scale=query[:, b : b + 1]
+                    dialogue_of_both(products[:], b),
+                    dialogue_of_both(bags[k][:], b),
+                    COPY,
+                    scale=query[:, b : b + 1],
                 )
-            nc.tensor.matmul(
-                scores[:], ones[:], products[:], start=(k == QUERY_BLOCKS[0]), stop=(k == QUERY_BLOCKS[-1])
-            )
+            for a in range(PARITIES):
+                nc.tensor.matmul(
+                    scores[:],
+                    ones[:],
+                    products[:, sum_of(a)],
+                    start=(k == QUERY_BLOCKS[0] and a == 0),
+                    stop=(k == QUERY_BLOCKS[-1] and a == PARITIES - 1),
+                )
 
         negative_max = held.tile([P, DIALOGUES], F32, name="negative_max")
         nc.vector.tensor_reduce(negative_max[:], by_dialogue(scores[:]), INNERMOST, MAX, negate=True)
@@ -125,11 +152,12 @@ def tile_encoder_kernel(tc, x, offs, out):
 
         k = VALUE_BLOCKS[0]
         sum_bag(k)
-        flipped_bag_psum = psum.tile([P, PIECE], F32, name="flipped_bag_psum")
-        for c in range(PAIRS):
-            nc.tensor.transpose(flipped_bag_psum[:, slots_of_pair(c)], bags[k][:, slots_of_pair(c)], identity[:])
-        flipped_bag = held.tile([P, PIECE], F32, name="flipped_bag")
-        nc.scalar.copy(flipped_bag[:], flipped_bag_psum[:])
+        flipped_bag = held.tile([P, PARITIES * PIECE], F32, name="flipped_bag")
+        for a in range(PARITIES):
+            flipped_bag_psum = psum.tile([P, PIECE], F32, name=f"flipped_bag_psum{a}")
+            for c in range(PAIRS):
+                nc.tensor.transpose(flipped_bag_psum[:, slots_of_pair(c)], bags[k][:, slots_of_pair(c, a)], identity[:])
+            nc.scalar.copy(flipped_bag[:, sum_of(a)], flipped_bag_psum[:])
         attention_column = psum.tile([P, PAIRS], F32, name="attention_column")
         for c in range(PAIRS):
             nc.tensor.matmul(
@@ -141,9 +169,14 @@ def tile_encoder_kernel(tc, x, offs, out):
         encoded_psum = psum.tile([P, DIALOGUES], F32, name="encoded_psum")
         for c in range(PAIRS):
             pair = slice(c * PAIR, (c + 1) * PAIR)
-            nc.tensor.matmul(
-                encoded_psum[:, pair], flipped_bag[:, slots_of_pair(c)], flipped_attention[:, pair], start=True, stop=True
-            )
+            for a in range(PARITIES):
+                nc.tensor.matmul(
+                    encoded_psum[:, pair],
+                    flipped_bag[:, slots_of_pair(c, a)],
+                    flipped_attention[:, pair],
+                    start=(a == 0),
+                    stop=(a == PARITIES - 1),
+                )
         nc.scalar.copy(encoded[k][:], encoded_psum[:])
         store(k)
 

@@ -22,6 +22,7 @@ LAST_BLOCK = BLOCKS[-1]
 PARITIES = 2
 PAIR = P // SLOTS
 PAIRS = DIALOGUES // PAIR
+GROUP = P // DIALOGUES
 
 FLOPS = 512 * (WORDS - 1) * PIECE + 256 * PIECE + 2 * 256 * PIECE + 2 * 256 * PIECE
 
@@ -36,10 +37,6 @@ def dialogue_of_both(flat, b):
 
 def slots_of(b):
     return slice(b * SLOTS, (b + 1) * SLOTS)
-
-
-def sum_of(a):
-    return slice(a * PIECE, (a + 1) * PIECE)
 
 
 def slots_of_pair(c, a=0):
@@ -60,14 +57,16 @@ def tile_encoder_kernel(tc, x, offs, out):
             nc.sync.dma_start(table[:], x[k * P : (k + 1) * P, :])
             tables.append(table)
 
-        ones = held.tile([P, P], BF16, name="ones")
+        to_group = held.tile([P, DIALOGUES * P], BF16, name="to_group")
+        nc.vector.memset(to_group[:], 0.0)
+        for b in range(DIALOGUES):
+            nc.vector.memset(to_group[:, b * P + b * GROUP : b * P + (b + 1) * GROUP], 1.0)
+        ones = held.tile([P, P], F32, name="ones")
         nc.vector.memset(ones[:], 1.0)
         zeros = held.tile([P, PIECE], F32, name="zeros")
         nc.vector.memset(zeros[:], 0.0)
         identity = held.tile([P, P], F32, name="identity")
         make_identity(nc, identity[:])
-        flipped_attention = held.tile([P, DIALOGUES], F32, name="flipped_attention")
-        nc.gpsimd.memset(flipped_attention[:], 0.0)
 
         span = {k: PIECE if k == LAST_BLOCK else PARITIES * PIECE for k in BLOCKS}
         steps = {k: WORDS * PIECE // span[k] for k in BLOCKS}
@@ -94,7 +93,7 @@ def tile_encoder_kernel(tc, x, offs, out):
                 for first in (0, span[k] // 2):
                     look_up(k, step, first, span[k] // 2)
 
-        scores = psum.tile([P, PIECE], F32, name="scores")
+        scores = psum.tile([P, SLOTS], F32, name="scores")
         for k in QUERY_BLOCKS:
             sum_bag(k)
             query = held.tile([P, DIALOGUES], F32, name=f"query{k}")
@@ -116,33 +115,31 @@ def tile_encoder_kernel(tc, x, offs, out):
                     scale=query[:, b : b + 1],
                 )
             for a in range(PARITIES):
-                nc.tensor.matmul(
-                    scores[:],
-                    ones[:],
-                    products[:, sum_of(a)],
-                    start=(k == QUERY_BLOCKS[0] and a == 0),
-                    stop=(k == QUERY_BLOCKS[-1] and a == PARITIES - 1),
-                )
+                for b in range(DIALOGUES):
+                    nc.tensor.matmul(
+                        scores[:],
+                        to_group[:, b * P : (b + 1) * P],
+                        products[:, a * PIECE + b * SLOTS : a * PIECE + (b + 1) * SLOTS],
+                        start=(k == QUERY_BLOCKS[0] and a == 0 and b == 0),
+                        stop=(k == QUERY_BLOCKS[-1] and a == PARITIES - 1 and b == DIALOGUES - 1),
+                    )
 
-        negative_max = held.tile([P, DIALOGUES], F32, name="negative_max")
-        nc.vector.tensor_reduce(negative_max[:], by_dialogue(scores[:]), INNERMOST, MAX, negate=True)
-        weights = held.tile([P, PIECE], F32, name="weights")
-        weight_sum = held.tile([P, DIALOGUES], F32, name="weight_sum")
-        for b in range(DIALOGUES):
-            nc.scalar.activation(
-                weights[:, slots_of(b)],
-                scores[:, slots_of(b)],
-                EXP,
-                bias=negative_max[:, b : b + 1],
-                accum_out=weight_sum[:, b : b + 1],
-            )
-        inverse_sum = held.tile([P, DIALOGUES], F32, name="inverse_sum")
+        negative_max = held.tile([P, 1], F32, name="negative_max")
+        nc.vector.tensor_reduce(negative_max[:], scores[:], INNERMOST, MAX, negate=True)
+        weights = held.tile([P, SLOTS], F32, name="weights")
+        weight_sum = held.tile([P, 1], F32, name="weight_sum")
+        nc.scalar.activation(weights[:], scores[:], EXP, bias=negative_max[:], accum_out=weight_sum[:])
+        inverse_sum = held.tile([P, 1], F32, name="inverse_sum")
         nc.vector.reciprocal(inverse_sum[:], weight_sum[:])
-        attention = held.tile([P, PIECE], F32, name="attention")
+        share = held.tile([P, DIALOGUES], F32, name="share")
+        nc.scalar.activation(share[:], identity[:, ::GROUP], COPY, scale=inverse_sum[:])
+        spread = held.tile([P, PIECE], F32, name="spread")
         for b in range(DIALOGUES):
-            nc.scalar.activation(
-                attention[:, slots_of(b)], weights[:, slots_of(b)], COPY, scale=inverse_sum[:, b : b + 1]
-            )
+            nc.scalar.activation(spread[:, slots_of(b)], weights[:], COPY, scale=share[:, b : b + 1])
+        attention_psum = psum.tile([P, PIECE], F32, name="attention_psum")
+        nc.tensor.matmul(attention_psum[:], ones[:], spread[:], start=True, stop=True)
+        attention = held.tile([P, PIECE], F32, name="attention")
+        nc.scalar.copy(attention[:], attention_psum[:])
 
         encoded = {k: held.tile([P, DIALOGUES], F32, name=f"encoded{k}") for k in VALUE_BLOCKS}
 
@@ -152,31 +149,38 @@ def tile_encoder_kernel(tc, x, offs, out):
 
         k = VALUE_BLOCKS[0]
         sum_bag(k)
-        flipped_bag = held.tile([P, PARITIES * PIECE], F32, name="flipped_bag")
-        for a in range(PARITIES):
-            flipped_bag_psum = psum.tile([P, PIECE], F32, name=f"flipped_bag_psum{a}")
-            for c in range(PAIRS):
-                nc.tensor.transpose(flipped_bag_psum[:, slots_of_pair(c)], bags[k][:, slots_of_pair(c, a)], identity[:])
-            nc.scalar.copy(flipped_bag[:, sum_of(a)], flipped_bag_psum[:])
-        attention_column = psum.tile([P, PAIRS], F32, name="attention_column")
+        flipped_bag_psum = psum.tile([P, PIECE], F32, name="flipped_bag_psum")
         for c in range(PAIRS):
-            nc.tensor.matmul(
-                attention_column[:, c : c + 1], attention[:, slots_of_pair(c)], identity[:, 0:1], start=True, stop=True
-            )
-        for h in range(PAIR):
-            slots_of_half = slice(h * SLOTS, (h + 1) * SLOTS)
-            nc.scalar.copy(flipped_attention[slots_of_half, h::PAIR], attention_column[slots_of_half, :])
-        encoded_psum = psum.tile([P, DIALOGUES], F32, name="encoded_psum")
-        for c in range(PAIRS):
-            pair = slice(c * PAIR, (c + 1) * PAIR)
             for a in range(PARITIES):
                 nc.tensor.matmul(
-                    encoded_psum[:, pair],
-                    flipped_bag[:, slots_of_pair(c, a)],
-                    flipped_attention[:, pair],
+                    flipped_bag_psum[:, slots_of_pair(c)],
+                    bags[k][:, slots_of_pair(c, a)],
+                    identity[:],
                     start=(a == 0),
                     stop=(a == PARITIES - 1),
                 )
+        flipped_bag = held.tile([P, PIECE], F32, name="flipped_bag")
+        nc.scalar.copy(flipped_bag[:], flipped_bag_psum[:])
+        flipped_attention_psum = psum.tile([P, PAIRS * DIALOGUES], F32, name="flipped_attention_psum")
+        for c in range(PAIRS):
+            nc.tensor.matmul(
+                flipped_attention_psum[:, c * DIALOGUES : (c + 1) * DIALOGUES],
+                spread[:, slots_of_pair(c)],
+                identity[:, ::GROUP],
+                start=True,
+                stop=True,
+            )
+        flipped_attention = held.tile([P, PAIRS * DIALOGUES], F32, name="flipped_attention")
+        nc.scalar.copy(flipped_attention[:], flipped_attention_psum[:])
+        encoded_psum = psum.tile([P, DIALOGUES], F32, name="encoded_psum")
+        for c in range(PAIRS):
+            nc.tensor.matmul(
+                encoded_psum[:],
+                flipped_bag[:, slots_of_pair(c)],
+                flipped_attention[:, c * DIALOGUES : (c + 1) * DIALOGUES],
+                start=(c == 0),
+                stop=(c == PAIRS - 1),
+            )
         nc.scalar.copy(encoded[k][:], encoded_psum[:])
         store(k)
 

@@ -158,6 +158,7 @@ def tile_encoder_kernel(tc, x, offs, out):
                     identity[:],
                     start=(a == 0),
                     stop=(a == PARITIES - 1),
+                    is_transpose=True,
                 )
         flipped_bag = held.tile([P, PIECE], F32, name="flipped_bag")
         nc.scalar.copy(flipped_bag[:], flipped_bag_psum[:])

@@ -20,9 +20,11 @@ VALUE_BLOCKS = (2, 3)
 BLOCKS = QUERY_BLOCKS + VALUE_BLOCKS
 LAST_BLOCK = BLOCKS[-1]
 PARITIES = 2
+LINKS = WORDS // PARITIES
 PAIR = P // SLOTS
 PAIRS = DIALOGUES // PAIR
 GROUP = P // DIALOGUES
+ROW = SLOTS + 4
 
 FLOPS = 512 * (WORDS - 1) * PIECE + 256 * PIECE + 2 * 256 * PIECE + 2 * 256 * PIECE
 
@@ -67,42 +69,46 @@ def tile_encoder_kernel(tc, x, offs, out):
         nc.vector.memset(zeros[:], 0.0)
         identity = held.tile([P, P], F32, name="identity")
         make_identity(nc, identity[:])
+        heads = identity[:, ::GROUP]
+        flipped_attention = held.tile([P, PAIRS * DIALOGUES], F32, name="flipped_attention")
+        nc.gpsimd.memset(flipped_attention[:], 0.0)
 
-        span = {k: PIECE if k == LAST_BLOCK else PARITIES * PIECE for k in BLOCKS}
-        steps = {k: WORDS * PIECE // span[k] for k in BLOCKS}
-        sums = [[held.tile([P, span[k]], F32, name=f"sum{k}_{i}") for i in range(2)] for k in BLOCKS]
-        bags = [sums[k][(steps[k] - 1) % 2] for k in BLOCKS]
+        written = {}
+        for k in BLOCKS:
+            two = [held.tile([P, PARITIES * PIECE], F32, name=f"sums{k}_{i}") for i in range(2)]
+            written[k] = [two[i % 2] for i in range(LINKS)]
 
-        def look_up(k, step, first, width):
-            columns = slice(first, first + width)
-            entry = step * span[k] + first
-            picked = tables[k][:].indirect(offsets[:, entry // 16 : (entry + width) // 16])
-            if entry == 0:
-                nc.vector.tensor_copy(sums[k][0][:, columns], picked)
-            elif step == 0:
-                nc.vector.tensor_tensor(sums[k][0][:, columns], picked, zeros[:], ADD)
-            else:
-                nc.vector.tensor_tensor(
-                    sums[k][step % 2][:, columns], picked, sums[k][(step - 1) % 2][:, columns], ADD
-                )
+        def look_up(k, t, a, i, first=0, stop=PIECE):
+            columns = slice(a * PIECE + first, a * PIECE + stop)
+            entry = t * PIECE + first
+            nc.vector.tensor_tensor(
+                written[k][i][:, columns],
+                tables[k][:].indirect(offsets[:, entry // 16 : (entry + stop - first) // 16]),
+                written[k][i - 1][:, columns] if i else zeros[:, first:stop],
+                ADD,
+            )
 
         def sum_bag(k):
-            for first in range(0, span[k], PIECE):
-                look_up(k, 0, first, PIECE)
-            for step in range(1, steps[k]):
-                for first in (0, span[k] // 2):
-                    look_up(k, step, first, span[k] // 2)
+            for i in range(LINKS):
+                for a in range(PARITIES):
+                    look_up(k, PARITIES * i + a, a, i)
+            return written[k][-1]
 
         scores = psum.tile([P, SLOTS], F32, name="scores")
         for k in QUERY_BLOCKS:
-            sum_bag(k)
+            bag = sum_bag(k)
             query = held.tile([P, DIALOGUES], F32, name=f"query{k}")
             discarded = held.tile([P, PARITIES * PIECE], BF16, name=f"discarded{k}")
-            products = held.tile([P, PARITIES * PIECE], BF16, name=f"products{k}")
+            products = held.tile(
+                [P, PARITIES * PIECE],
+                BF16,
+                name=f"products{k}",
+                tag="late" if k == QUERY_BLOCKS[-1] else f"products{k}",
+            )
             for b in range(DIALOGUES):
                 nc.scalar.activation(
                     dialogue_of_both(discarded[:], b),
-                    dialogue_of_both(bags[k][:], b),
+                    dialogue_of_both(bag[:], b),
                     COPY,
                     scale=1.0 / SLOTS,
                     accum_out=query[:, b : b + 1],
@@ -110,12 +116,11 @@ def tile_encoder_kernel(tc, x, offs, out):
             for b in range(DIALOGUES):
                 nc.scalar.activation(
                     dialogue_of_both(products[:], b),
-                    dialogue_of_both(bags[k][:], b),
+                    dialogue_of_both(bag[:], b),
                     COPY,
                     scale=query[:, b : b + 1],
                 )
-            for a in range(PARITIES):
-                for b in range(DIALOGUES):
+                for a in range(PARITIES):
                     nc.tensor.matmul(
                         scores[:],
                         to_group[:, b * P : (b + 1) * P],
@@ -131,13 +136,25 @@ def tile_encoder_kernel(tc, x, offs, out):
         nc.scalar.activation(weights[:], scores[:], EXP, bias=negative_max[:], accum_out=weight_sum[:])
         inverse_sum = held.tile([P, 1], F32, name="inverse_sum")
         nc.vector.reciprocal(inverse_sum[:], weight_sum[:])
-        share = held.tile([P, DIALOGUES], F32, name="share")
-        nc.scalar.activation(share[:], identity[:, ::GROUP], COPY, scale=inverse_sum[:])
+        weights_twice = held.tile([P, PAIR * SLOTS], F32, name="weights_twice")
+        nc.scalar.copy(by_dialogue(weights_twice[:]), weights[:].unsqueeze(1).to_broadcast([P, PAIR, SLOTS]))
         spread = held.tile([P, PIECE], F32, name="spread")
         for b in range(DIALOGUES):
-            nc.scalar.activation(spread[:, slots_of(b)], weights[:], COPY, scale=share[:, b : b + 1])
+            nc.scalar.activation(spread[:, slots_of(b)], weights[:], COPY, scale=heads[:, b : b + 1])
+        share = held.tile([P, DIALOGUES], F32, name="share")
+        nc.scalar.activation(share[:], heads, COPY, scale=inverse_sum[:])
+        shares = held.tile([P, P], F32, name="shares")
+        nc.scalar.activation(shares[:], ones[:], COPY, scale=inverse_sum[:])
+        flipped_attention_psum = psum.tile([P, DIALOGUES], F32, name="flipped_attention_psum")
+        nc.tensor.matmul(flipped_attention_psum[:], weights_twice[:], share[:], start=True, stop=True)
+        for i in range(PAIR):
+            half = slice(i * SLOTS, (i + 1) * SLOTS)
+            nc.scalar.copy(
+                flipped_attention[half, i :: DIALOGUES + PAIR],
+                flipped_attention_psum[half, i::PAIR],
+            )
         attention_psum = psum.tile([P, PIECE], F32, name="attention_psum")
-        nc.tensor.matmul(attention_psum[:], ones[:], spread[:], start=True, stop=True)
+        nc.tensor.matmul(attention_psum[:], shares[:], spread[:], start=True, stop=True)
         attention = held.tile([P, PIECE], F32, name="attention")
         nc.scalar.copy(attention[:], attention_psum[:])
 
@@ -147,55 +164,61 @@ def tile_encoder_kernel(tc, x, offs, out):
             first_row = (k - VALUE_BLOCKS[0]) * P
             nc.sync.dma_start(out[first_row : first_row + P, :], encoded[k][:])
 
-        k = VALUE_BLOCKS[0]
-        sum_bag(k)
-        flipped_bag_psum = psum.tile([P, PIECE], F32, name="flipped_bag_psum")
-        for c in range(PAIRS):
-            for a in range(PARITIES):
+        def encode(k, bag, parities):
+            flipped = held.tile([P, PIECE], F32, name=f"flipped{k}")
+            for c in range(PAIRS):
+                flipped_pair = psum.tile([P, P], F32, name=f"flipped_pair{k}_{c}", tag=f"flipped_pair{c}")
+                for a in parities:
+                    nc.tensor.matmul(
+                        flipped_pair[:],
+                        bag[:, slots_of_pair(c, a)],
+                        identity[:],
+                        start=(a == parities[0]),
+                        stop=(a == parities[-1]),
+                        is_transpose=True,
+                    )
+                nc.scalar.copy(flipped[:, slots_of_pair(c)], flipped_pair[:])
+            encoded_psum = psum.tile([P, DIALOGUES], F32, name=f"encoded_psum{k}", tag="encoded_psum")
+            for c in range(PAIRS):
                 nc.tensor.matmul(
-                    flipped_bag_psum[:, slots_of_pair(c)],
-                    bags[k][:, slots_of_pair(c, a)],
-                    identity[:],
-                    start=(a == 0),
-                    stop=(a == PARITIES - 1),
-                    is_transpose=True,
+                    encoded_psum[:],
+                    flipped[:, slots_of_pair(c)],
+                    flipped_attention[:, c * DIALOGUES : (c + 1) * DIALOGUES],
+                    start=(c == 0),
+                    stop=(c == PAIRS - 1),
                 )
-        flipped_bag = held.tile([P, PIECE], F32, name="flipped_bag")
-        nc.scalar.copy(flipped_bag[:], flipped_bag_psum[:])
-        flipped_attention_psum = psum.tile([P, PAIRS * DIALOGUES], F32, name="flipped_attention_psum")
-        for c in range(PAIRS):
-            nc.tensor.matmul(
-                flipped_attention_psum[:, c * DIALOGUES : (c + 1) * DIALOGUES],
-                spread[:, slots_of_pair(c)],
-                identity[:, ::GROUP],
-                start=True,
-                stop=True,
-            )
-        flipped_attention = held.tile([P, PAIRS * DIALOGUES], F32, name="flipped_attention")
-        nc.scalar.copy(flipped_attention[:], flipped_attention_psum[:])
-        encoded_psum = psum.tile([P, DIALOGUES], F32, name="encoded_psum")
-        for c in range(PAIRS):
-            nc.tensor.matmul(
-                encoded_psum[:],
-                flipped_bag[:, slots_of_pair(c)],
-                flipped_attention[:, c * DIALOGUES : (c + 1) * DIALOGUES],
-                start=(c == 0),
-                stop=(c == PAIRS - 1),
-            )
-        nc.scalar.copy(encoded[k][:], encoded_psum[:])
+            return encoded_psum
+
+        k = VALUE_BLOCKS[0]
+        written[k][2] = held.tile([P, PARITIES * PIECE], F32, name="late", tag="late")
+        written[k][3] = written[k][0]
+        nc.scalar.copy(encoded[k][:], encode(k, sum_bag(k), (0, 1))[:])
         store(k)
 
-        k = VALUE_BLOCKS[1]
-        sum_bag(k)
-        weighted = held.tile([P, PIECE], F32, name="weighted")
-        halves = (slice(0, PIECE // 2), slice(PIECE // 2, PIECE))
-        for half in halves:
-            nc.vector.tensor_tensor(weighted[:, half], bags[k][:, half], attention[:, half], MULT)
-        for half in halves:
-            nc.vector.tensor_reduce(
-                encoded[k][:, half.start // SLOTS : half.stop // SLOTS],
-                by_dialogue(weighted[:, half]),
-                INNERMOST,
-                ADD,
+        k = LAST_BLOCK
+        odd, even = 1, 0
+        for i in range(2):
+            look_up(k, 2 * i + 1, odd, i)
+            look_up(k, 2 * i, even, i)
+        look_up(k, 5, odd, 2)
+        weighted = held.tile([P, DIALOGUES * ROW], F32, name="weighted")
+        rows = weighted[:].rearrange("p (b m) -> p b m", m=ROW)
+        nc.scalar.copy(rows[:, :, SLOTS : SLOTS + 1], encode(k, written[k][2], (odd,))[:].unsqueeze(2))
+        written[k].append(written[k][0])
+        for i, t in ((2, 4), (3, 6), (4, 7)):
+            for first in (0, PIECE // 2):
+                look_up(k, t, even, i, first, first + PIECE // 2)
+        even_sum, attention_rows = by_dialogue(written[k][4][:, :PIECE]), by_dialogue(attention[:])
+        first_part, second_part, third_part = slice(0, 3), slice(3, 5), slice(5, 8)
+        for part in (first_part, second_part, third_part):
+            nc.vector.tensor_tensor(
+                rows[:, part, :SLOTS], even_sum[:, part, :], attention_rows[:, part, :], MULT
             )
+        summed = held.tile([P, ROW], F32, name="summed")
+        for b in range(first_part.start, first_part.stop):
+            nc.scalar.activation(
+                summed[:, : SLOTS + 1], rows[:, b, : SLOTS + 1], COPY, accum_out=encoded[k][:, b : b + 1]
+            )
+        for part in (second_part, third_part):
+            nc.vector.tensor_reduce(encoded[k][:, part], rows[:, part, : SLOTS + 1], INNERMOST, ADD)
         store(k)

@@ -209,16 +209,11 @@ def tile_encoder_kernel(tc, x, offs, out):
             for first in (0, PIECE // 2):
                 look_up(k, t, even, i, first, first + PIECE // 2)
         even_sum, attention_rows = by_dialogue(written[k][4][:, :PIECE]), by_dialogue(attention[:])
-        first_part, second_part, third_part = slice(0, 3), slice(3, 5), slice(5, 8)
-        for part in (first_part, second_part, third_part):
+        halves = (slice(0, DIALOGUES // 2), slice(DIALOGUES // 2, DIALOGUES))
+        for half in halves:
             nc.vector.tensor_tensor(
-                rows[:, part, :SLOTS], even_sum[:, part, :], attention_rows[:, part, :], MULT
+                rows[:, half, :SLOTS], even_sum[:, half, :], attention_rows[:, half, :], MULT
             )
-        summed = held.tile([P, ROW], F32, name="summed")
-        for b in range(first_part.start, first_part.stop):
-            nc.scalar.activation(
-                summed[:, : SLOTS + 1], rows[:, b, : SLOTS + 1], COPY, accum_out=encoded[k][:, b : b + 1]
-            )
-        for part in (second_part, third_part):
-            nc.vector.tensor_reduce(encoded[k][:, part], rows[:, part, : SLOTS + 1], INNERMOST, ADD)
+        for half in halves:
+            nc.vector.tensor_reduce(encoded[k][:, half], rows[:, half, : SLOTS + 1], INNERMOST, ADD)
         store(k)

@@ -81,12 +81,12 @@ def tile_encoder_kernel(tc, x, offs, out):
         def look_up(k, t, a, i, first=0, stop=PIECE):
             columns = slice(a * PIECE + first, a * PIECE + stop)
             entry = t * PIECE + first
-            nc.vector.tensor_tensor(
-                written[k][i][:, columns],
-                tables[k][:].indirect(offsets[:, entry // 16 : (entry + stop - first) // 16]),
-                written[k][i - 1][:, columns] if i else zeros[:, first:stop],
-                ADD,
-            )
+            picked = tables[k][:].indirect(offsets[:, entry // 16 : (entry + stop - first) // 16])
+            if t == 0:
+                nc.vector.tensor_copy(written[k][i][:, columns], picked)
+            else:
+                source = written[k][i - 1][:, columns] if i else zeros[:, first:stop]
+                nc.vector.tensor_tensor(written[k][i][:, columns], picked, source, ADD)
 
         def sum_bag(k):
             for i in range(LINKS):
@@ -99,12 +99,7 @@ def tile_encoder_kernel(tc, x, offs, out):
             bag = sum_bag(k)
             query = held.tile([P, DIALOGUES], F32, name=f"query{k}")
             discarded = held.tile([P, PARITIES * PIECE], BF16, name=f"discarded{k}")
-            products = held.tile(
-                [P, PARITIES * PIECE],
-                BF16,
-                name=f"products{k}",
-                tag="late" if k == QUERY_BLOCKS[-1] else f"products{k}",
-            )
+            products = held.tile([P, PARITIES * PIECE], BF16, name=f"products{k}")
             for b in range(DIALOGUES):
                 nc.scalar.activation(
                     dialogue_of_both(discarded[:], b),
@@ -120,7 +115,8 @@ def tile_encoder_kernel(tc, x, offs, out):
                     COPY,
                     scale=query[:, b : b + 1],
                 )
-                for a in range(PARITIES):
+            for a in range(PARITIES):
+                for b in range(DIALOGUES):
                     nc.tensor.matmul(
                         scores[:],
                         to_group[:, b * P : (b + 1) * P],
@@ -190,8 +186,6 @@ def tile_encoder_kernel(tc, x, offs, out):
             return encoded_psum
 
         k = VALUE_BLOCKS[0]
-        written[k][2] = held.tile([P, PARITIES * PIECE], F32, name="late", tag="late")
-        written[k][3] = written[k][0]
         nc.scalar.copy(encoded[k][:], encode(k, sum_bag(k), (0, 1))[:])
         store(k)
 

import concourse.mybir as mybir
from concourse.masks import make_identity

F32 = mybir.dt.float32
BF16 = mybir.dt.bfloat16
U16 = mybir.dt.uint16
ADD = mybir.AluOpType.add
MULT = mybir.AluOpType.mult
MAX = mybir.AluOpType.max
EXP = mybir.ActivationFunctionType.Exp
COPY = mybir.ActivationFunctionType.Copy
INNERMOST = mybir.AxisListType.X

P = 128
VOCAB = 4096
WORDS, DIALOGUES, SLOTS = 8, 8, 64
PIECE = DIALOGUES * SLOTS
QUERY_BLOCKS = (0, 1)
VALUE_BLOCKS = (2, 3)
BLOCKS = QUERY_BLOCKS + VALUE_BLOCKS
LAST_BLOCK = BLOCKS[-1]
PARITIES = 2
LINKS = WORDS // PARITIES
PAIR = P // SLOTS
PAIRS = DIALOGUES // PAIR
GROUP = P // DIALOGUES
ROW = SLOTS + 4

FLOPS = 512 * (WORDS - 1) * PIECE + 256 * PIECE + 2 * 256 * PIECE + 2 * 256 * PIECE


def by_dialogue(flat):
    return flat.rearrange("p (b m) -> p b m", m=SLOTS)


def dialogue_of_both(flat, b):
    return flat.rearrange("p (a b m) -> p a b m", a=PARITIES, m=SLOTS)[:, :, b : b + 1, :]


def slots_of(b):
    return slice(b * SLOTS, (b + 1) * SLOTS)


def slots_of_pair(c, a=0):
    return slice(a * PIECE + c * P, a * PIECE + (c + 1) * P)


def tile_encoder_kernel(tc, x, offs, out):
    nc = tc.nc
    with (
        tc.tile_pool(name="held", bufs=1) as held,
        tc.psum_pool(name="psum", bufs=1) as psum,
    ):
        offsets = held.tile([P, WORDS * PIECE // 16], U16, name="offsets")
        nc.sync.dma_start(offsets[:], offs)
        tables = []
        for k in BLOCKS:
            table = held.tile([P, VOCAB], F32, name=f"table{k}")
            nc.sync.dma_start(table[:], x[k * P : (k + 1) * P, :])
            tables.append(table)

        to_group = held.tile([P, DIALOGUES * P], BF16, name="to_group")
        nc.vector.memset(to_group[:], 0.0)
        for b in range(DIALOGUES):
            nc.vector.memset(to_group[:, b * P + b * GROUP : b * P + (b + 1) * GROUP], 1.0)
        ones = held.tile([P, P], F32, name="ones")
        nc.vector.memset(ones[:], 1.0)
        zeros = held.tile([P, PIECE], F32, name="zeros")
        nc.vector.memset(zeros[:], 0.0)
        identity = held.tile([P, P], F32, name="identity")
        make_identity(nc, identity[:])
        heads = identity[:, ::GROUP]
        flipped_attention = held.tile([P, PAIRS * DIALOGUES], F32, name="flipped_attention")
        nc.gpsimd.memset(flipped_attention[:], 0.0)

        written = {}
        for k in BLOCKS:
            two = [held.tile([P, PARITIES * PIECE], F32, name=f"sums{k}_{i}") for i in range(2)]
            written[k] = [two[i % 2] for i in range(LINKS)]

        def look_up(k, t, a, i, first=0, stop=PIECE):
            columns = slice(a * PIECE + first, a * PIECE + stop)
            entry = t * PIECE + first
            picked = tables[k][:].indirect(offsets[:, entry // 16 : (entry + stop - first) // 16])
            if t == 0:
                nc.vector.tensor_copy(written[k][i][:, columns], picked)
            else:
                source = written[k][i - 1][:, columns] if i else zeros[:, first:stop]
                nc.vector.tensor_tensor(written[k][i][:, columns], picked, source, ADD)

        def sum_bag(k):
            for i in range(LINKS):
                for a in range(PARITIES):
                    look_up(k, PARITIES * i + a, a, i)
            return written[k][-1]

        scores = psum.tile([P, SLOTS], F32, name="scores")
        for k in QUERY_BLOCKS:
            bag = sum_bag(k)
            query = held.tile([P, DIALOGUES], F32, name=f"query{k}")
            discarded = held.tile([P, PARITIES * PIECE], BF16, name=f"discarded{k}")
            products = held.tile([P, PARITIES * PIECE], BF16, name=f"products{k}")
            for b in range(DIALOGUES):
                nc.scalar.activation(
                    dialogue_of_both(discarded[:], b),
                    dialogue_of_both(bag[:], b),
                    COPY,
                    scale=1.0 / SLOTS,
                    accum_out=query[:, b : b + 1],
                )
            for b in range(DIALOGUES):
                nc.scalar.activation(
                    dialogue_of_both(products[:], b),
                    dialogue_of_both(bag[:], b),
                    COPY,
                    scale=query[:, b : b + 1],
                )
            for a in range(PARITIES):
                for b in range(DIALOGUES):
                    nc.tensor.matmul(
                        scores[:],
                        to_group[:, b * P : (b + 1) * P],
                        products[:, a * PIECE + b * SLOTS : a * PIECE + (b + 1) * SLOTS],
                        start=(k == QUERY_BLOCKS[0] and a == 0 and b == 0),
                        stop=(k == QUERY_BLOCKS[-1] and a == PARITIES - 1 and b == DIALOGUES - 1),
                    )

        negative_max = held.tile([P, 1], F32, name="negative_max")
        nc.vector.tensor_reduce(negative_max[:], scores[:], INNERMOST, MAX, negate=True)
        weights = held.tile([P, SLOTS], F32, name="weights")
        weight_sum = held.tile([P, 1], F32, name="weight_sum")
        nc.scalar.activation(weights[:], scores[:], EXP, bias=negative_max[:], accum_out=weight_sum[:])
        inverse_sum = held.tile([P, 1], F32, name="inverse_sum")
        nc.vector.reciprocal(inverse_sum[:], weight_sum[:])
        weights_twice = held.tile([P, PAIR * SLOTS], F32, name="weights_twice")
        nc.scalar.copy(by_dialogue(weights_twice[:]), weights[:].unsqueeze(1).to_broadcast([P, PAIR, SLOTS]))
        spread = held.tile([P, PIECE], F32, name="spread")
        for b in range(DIALOGUES):
            nc.scalar.activation(spread[:, slots_of(b)], weights[:], COPY, scale=heads[:, b : b + 1])
        share = held.tile([P, DIALOGUES], F32, name="share")
        nc.scalar.activation(share[:], heads, COPY, scale=inverse_sum[:])
        shares = held.tile([P, P], F32, name="shares")
        nc.scalar.activation(shares[:], ones[:], COPY, scale=inverse_sum[:])
        flipped_attention_psum = psum.tile([P, DIALOGUES], F32, name="flipped_attention_psum")
        nc.tensor.matmul(flipped_attention_psum[:], weights_twice[:], share[:], start=True, stop=True)
        for i in range(PAIR):
            half = slice(i * SLOTS, (i + 1) * SLOTS)
            nc.scalar.copy(
                flipped_attention[half, i :: DIALOGUES + PAIR],
                flipped_attention_psum[half, i::PAIR],
            )
        attention_psum = psum.tile([P, PIECE], F32, name="attention_psum")
        nc.tensor.matmul(attention_psum[:], shares[:], spread[:], start=True, stop=True)
        attention = held.tile([P, PIECE], F32, name="attention")
        nc.scalar.copy(attention[:], attention_psum[:])

        encoded = {k: held.tile([P, DIALOGUES], F32, name=f"encoded{k}") for k in VALUE_BLOCKS}

        def store(k):
            first_row = (k - VALUE_BLOCKS[0]) * P
            nc.sync.dma_start(out[first_row : first_row + P, :], encoded[k][:])

        def encode(k, bag, parities):
            flipped = held.tile([P, PIECE], F32, name=f"flipped{k}")
            for c in range(PAIRS):
                flipped_pair = psum.tile([P, P], F32, name=f"flipped_pair{k}_{c}", tag=f"flipped_pair{c}")
                for a in parities:
                    nc.tensor.matmul(
                        flipped_pair[:],
                        bag[:, slots_of_pair(c, a)],
                        identity[:],
                        start=(a == parities[0]),
                        stop=(a == parities[-1]),
                        is_transpose=True,
                    )
                nc.scalar.copy(flipped[:, slots_of_pair(c)], flipped_pair[:])
            encoded_psum = psum.tile([P, DIALOGUES], F32, name=f"encoded_psum{k}", tag="encoded_psum")
            for c in range(PAIRS):
                nc.tensor.matmul(
                    encoded_psum[:],
                    flipped[:, slots_of_pair(c)],
                    flipped_attention[:, c * DIALOGUES : (c + 1) * DIALOGUES],
                    start=(c == 0),
                    stop=(c == PAIRS - 1),
                )
            return encoded_psum

        k = VALUE_BLOCKS[0]
        nc.scalar.copy(encoded[k][:], encode(k, sum_bag(k), (0, 1))[:])
        store(k)

        k = LAST_BLOCK
        odd, even = 1, 0
        for i in range(2):
            look_up(k, 2 * i + 1, odd, i)
            look_up(k, 2 * i, even, i)
        look_up(k, 5, odd, 2)
        weighted = held.tile([P, DIALOGUES * ROW], F32, name="weighted")
        rows = weighted[:].rearrange("p (b m) -> p b m", m=ROW)
        nc.scalar.copy(rows[:, :, SLOTS : SLOTS + 1], encode(k, written[k][2], (odd,))[:].unsqueeze(2))
        written[k].append(written[k][0])
        for i, t in ((2, 4), (3, 6), (4, 7)):
            for first in (0, PIECE // 2):
                look_up(k, t, even, i, first, first + PIECE // 2)
        even_sum, attention_rows = by_dialogue(written[k][4][:, :PIECE]), by_dialogue(attention[:])
        halves = (slice(0, DIALOGUES // 2), slice(DIALOGUES // 2, DIALOGUES))
        for half in halves:
            nc.vector.tensor_tensor(
                rows[:, half, :SLOTS], even_sum[:, half, :], attention_rows[:, half, :], MULT
            )
        for half in halves:
            nc.vector.tensor_reduce(encoded[k][:, half], rows[:, half, : SLOTS + 1], INNERMOST, ADD)
        store(k)
